import numpy as np
import ml_dtypes


def mxq(x, axis, fmt="e4m3"):
    dtype, down = {"e4m3": (ml_dtypes.float8_e4m3fn, 7), "e5m2": (ml_dtypes.float8_e5m2, 14)}[fmt]
    v = np.moveaxis(np.asarray(x, np.float32).astype(ml_dtypes.bfloat16).astype(np.float64), axis, -1)
    blocks = v.reshape(v.shape[:-1] + (-1, 32))
    amax = np.abs(blocks).max(-1, keepdims=True)
    byte = np.maximum(np.where(amax > 0, np.frexp(amax)[1] - 1 + 127, 0) - down, 1)
    scale = np.exp2(byte - 127.0)
    codes = (blocks / scale).astype(np.float32).astype(dtype).astype(np.float64)
    return np.moveaxis((codes * scale).reshape(v.shape), -1, axis)


WIDE = False


def mx_kscale(k):
    if not WIDE:
        return np.ones(k)
    levels = np.array([10, -10, 5, -5, 0])
    if k % 512:
        return np.exp2(np.random.permutation(np.resize(levels, k // 32))).repeat(32)
    a = np.empty((k // 512, 16))
    for p in range(k // 512):
        a[p, :8] = np.random.permutation(np.resize(levels, 8))
        for g in range(8):
            far = levels[np.abs(levels - a[p, g]) >= 10]
            a[p, g + 8] = far[np.random.randint(len(far))]
    return np.exp2(a.ravel()).repeat(32)


BF16 = ml_dtypes.bfloat16


def bf(x):
    return np.asarray(x, np.float32).astype(BF16)


def f64(x):
    return np.asarray(x).astype(np.float64)


B, U, F = 2048, 1024, 512


def sigmoid(v):
    return 1.0 / (1.0 + np.exp(-v))


def preact(x, shift, semi_axis, sharpness):
    x = f64(x)
    a = f64(semi_axis)
    s = f64(shift).reshape(a.shape)
    inv = 1.0 / np.square(a)
    quad = np.square(x) @ inv.T + 2.0 * (x @ (s * inv).T) + np.sum(np.square(s) * inv, axis=1)
    return (1.0 - quad) * f64(sharpness)


def setup_inputs():
    t = mx_kscale(B)[:, None]
    r = np.exp2(np.round(np.log2(mx_kscale(U)) / 2))
    c = np.square(r)
    m = np.min(t)
    x0 = bf(np.random.standard_normal((B, F)))
    shift0 = bf(np.random.standard_normal((U, F)))
    a0 = bf(np.sqrt(40.0 * F) * (0.1 + 0.4 * np.random.random_sample((U, F))))
    sharpness = bf(np.sqrt(F) * (0.5 + 0.5 * np.random.random_sample(U)))
    multiplier = bf(np.where(np.random.random_sample(U) > 0.5, 1.0, -1.0) * (1.0 + 0.1 * np.random.standard_normal(U)))
    g = bf(np.random.standard_normal((B, U)) * np.exp2(np.random.randint(-6, 1, (B, 1))) * 32.0 / t * c)
    z = preact(x0, shift0, a0, sharpness)
    return {"x": bf(f64(x0) * t), "shift": bf(f64(shift0) * m).reshape(U * F), "semi_axis": bf(f64(a0) * r[:, None]),
            "sharpness": sharpness, "multiplier": multiplier, "z": np.asarray(z, np.float32), "grad_out": g}


def reference(x, shift, semi_axis, sharpness, multiplier, z, grad_out):
    x = f64(x)
    a = f64(semi_axis)
    u, f = a.shape
    s = f64(shift).reshape(u, f)
    inv = 1.0 / np.square(a)
    p = sigmoid(f64(z))
    dq = -f64(grad_out) * (f64(multiplier) * f64(sharpness)) * (p * (1.0 - p))
    w = np.concatenate([inv, s * inv], axis=1)
    pr = mxq(dq, 1, "e5m2") @ mxq(w, 0, "e4m3")
    dx = 2.0 * (x * pr[:, :f] + pr[:, f:])
    gm = mxq(dq, 0, "e5m2").T @ mxq(x, 0, "e4m3")
    ds = 2.0 * inv * (gm + s * np.sum(dq, axis=0)[:, None])
    return dx, ds.reshape(u * f)

from contextlib import ExitStack

import concourse.mybir as mybir
from concourse.masks import make_identity

B, U, F = 2048, 1024, 512
FLOPS = 2 * B * U * 2 * F + 2 * B * U * F

F32 = mybir.dt.float32
BF16 = mybir.dt.bfloat16
U32 = mybir.dt.uint32
U8 = mybir.dt.uint8
E4 = mybir.dt.float8_e4m3fn_x4
E5 = mybir.dt.float8_e5m2_x4
ACT = mybir.ActivationFunctionType
ALU = mybir.AluOpType
AX = mybir.AxisListType

P = 128
NH = 2
NG = 4
H = U // NH

GP_SLOTS = {0: (), 1: (3,)}


def tile_boundedparaboloids_v_kernel(tc, x, shift, semi_axis, sharpness, multiplier, z, grad_out, out_0, out_1):
    nc = tc.nc
    z_v = z.rearrange("(g p j) (h w) -> h g p j w", g=NG, p=P, j=4, h=NH)
    go_v = grad_out.rearrange("(g p j) (h w) -> h g p j w", g=NG, p=P, j=4, h=NH)
    x_v = x.rearrange("(g p j) f -> g p j f", g=NG, p=P, j=4)
    a_v = semi_axis.rearrange("(h q t e) f -> h e q t f", h=NH, q=64, t=4, e=2)
    s_v = shift.rearrange("(h q t e f) -> h e q t f", h=NH, q=64, t=4, e=2, f=F)
    o0_v = out_0.rearrange("(g p j) f -> g p j f", g=NG, p=P, j=4)
    o1_v = out_1.rearrange("(h q t e f) -> h e q t f", h=NH, q=64, t=4, e=2, f=F)

    with ExitStack() as ctx:
        keep = ctx.enter_context(tc.tile_pool(name="keep", bufs=1))
        ring = ctx.enter_context(tc.tile_pool(name="ring", bufs=2))
        psum = ctx.enter_context(tc.psum_pool(name="psum", bufs=1))

        ident_f = keep.tile([P, P], F32, name="ident_f")
        make_identity(nc, ident_f[:])
        ones = keep.tile([P, P], BF16, name="ones")
        nc.gpsimd.memset(ones[:], 1.0)

        mrow = keep.tile([1, U], BF16, name="mrow")
        srow = keep.tile([1, U], BF16, name="srow")
        nc.sync.dma_start(out=mrow[:], in_=multiplier.rearrange("(o u) -> o u", o=1))
        nc.sync.dma_start(out=srow[:], in_=sharpness.rearrange("(o u) -> o u", o=1))
        frow = keep.tile([1, U], F32, name="frow")
        f_hi = keep.tile([P, U], BF16, name="f_hi")
        f_lo = keep.tile([P, U], BF16, name="f_lo")
        nc.vector.memset(f_hi[:], 0.0)
        nc.vector.memset(f_lo[:], 0.0)
        nc.vector.scalar_tensor_tensor(out=frow[:], in0=mrow[:], scalar=0.25, in1=srow[:], op0=ALU.mult, op1=ALU.mult)
        for h in range(NH):
            for t in range(4):
                o = h * H + t * P
                src = frow[:, h * H : (h + 1) * H].rearrange("p (q t e) -> p t q e", q=64, t=4, e=2)[:, t]
                hi = f_hi[0:1, o : o + P].rearrange("p (q e) -> p q e", e=2)
                lo = f_lo[0:1, o : o + P].rearrange("p (q e) -> p q e", e=2)
                nc.vector.tensor_copy(out=hi, in_=src)
                nc.vector.tensor_tensor(out=lo, in0=src, in1=hi, op=ALU.subtract)
        f_col = keep.tile([P, 8], F32, name="f_col")
        fc_ps = psum.tile([P, 8, 2], F32, name="fc_ps", tag="sum")
        for i in range(8):
            nc.tensor.matmul(fc_ps[:, i, :], lhsT=f_hi[:, i * P : (i + 1) * P], rhs=ones[:, 0:2], start=True, stop=False)
            nc.tensor.matmul(fc_ps[:, i, :], lhsT=f_lo[:, i * P : (i + 1) * P], rhs=ones[:, 0:2], start=False, stop=True)
        nc.vector.tensor_copy(out=f_col[:], in_=fc_ps[:, :, 0])

        w_q, w_s, inv, s_sb, xq, xs, x_sb = {}, {}, {}, {}, {}, {}, {}
        q0, q0s, q1, q1s, tt_, f_ps, f_sb = {}, {}, {}, {}, {}, {}, {}

        def spread_f(h):
            f_ps[h] = psum.tile([P, H], F32, name="f_ps", tag="f_ps")
            nc.tensor.matmul(f_ps[h][:], lhsT=ones[:], rhs=f_hi[:, h * H : (h + 1) * H], start=True, stop=False)
            nc.tensor.matmul(f_ps[h][:], lhsT=ones[:], rhs=f_lo[:, h * H : (h + 1) * H], start=False, stop=True)
            if GP_SLOTS[h]:
                f_sb[h] = keep.tile([P, H], F32, name="f_sb")
                nc.scalar.copy(out=f_sb[h][:], in_=f_ps[h][:])

        zt, gt = {}, {}

        def load_chunk(h, g):
            zt[h, g] = ring.tile([P, 4, H], F32, name="zt", tag="zt", bufs=3)
            nc.sync.dma_start(out=zt[h, g][:], in_=z_v[h, g])
            gt[h, g] = ring.tile([P, 4, H], BF16, name="gt", tag="gt", bufs=3)
            nc.sync.dma_start(out=gt[h, g][:], in_=go_v[h, g])

        def load_x(g):
            x_sb[g] = keep.tile([P, 4, F], BF16, name="x_sb%d" % g)
            nc.sync.dma_start(out=x_sb[g][:], in_=x_v[g])

        def load_w(h):
            a_sb = ring.tile([P, 4, F], BF16, name="a_sb", tag="il", bufs=3, align_bytes=64)
            s_sb[h] = keep.tile([P, 4, F], BF16, name="s_sb%d" % h)
            for e in range(2):
                nc.sync.dma_start(out=a_sb[e:P:2, :, :], in_=a_v[h, e])
                nc.sync.dma_start(out=s_sb[h][e:P:2, :, :], in_=s_v[h, e])
            return a_sb

        def act_chunk(h, g):
            zz = zt[h, g]
            nc.scalar.activation(out=zz[:], in_=zz[:], func=ACT.Tanh, scale=0.5)
            nc.scalar.activation(out=zz[:], in_=zz[:], func=ACT.Square)

        def p1(h, g):
            t = ring.tile([P, 4, H], F32, name="t", tag="t", bufs=5)
            tt_[h, g] = t
            zv = zt[h, g][:].rearrange("p j (q t e) -> p t j q e", q=64, t=4, e=2)
            gv = gt[h, g][:].rearrange("p j (q t e) -> p t j q e", q=64, t=4, e=2)
            for k in range(4):
                nc.vector.scalar_tensor_tensor(
                    out=t[:, :, k * P : (k + 1) * P].rearrange("p j (q e) -> p j q e", e=2),
                    in0=zv[:, k], scalar=1.0, in1=gv[:, k], op0=ALU.subtract, op1=ALU.mult)

        dq = {}

        def p2(h, g):
            d = ring.tile([P, H, 4], BF16, name="d", tag="d", bufs=2, align_bytes=64)
            dq[h, g] = d
            gp = GP_SLOTS[h]
            nv = 4 - len(gp)
            tv = tt_[h, g][:].rearrange("p j c -> p c j")
            w = nv * P
            if nv:
                nc.vector.tensor_tensor(out=d[:, 0:w, :], in0=tv[:, 0:w, :],
                                        in1=f_ps[h][:, 0:w].unsqueeze(2).to_broadcast([P, w, 4]), op=ALU.mult)
            for k in gp:
                nc.gpsimd.tensor_tensor(out=d[:, k * P : (k + 1) * P, :], in0=tv[:, k * P : (k + 1) * P, :],
                                        in1=f_sb[h][:, k * P : (k + 1) * P].unsqueeze(2).to_broadcast([P, P, 4]), op=ALU.mult)

        def quant(src, fmt, name, bufs):
            codes = ring.tile([P, H], U32, name=name, tag=name, bufs=bufs, align_bytes=64)
            scales = ring.tile([P, H], U8, name=name + "s", tag=name + "s", bufs=bufs, align_bytes=64)
            nc.vector.quantize_mx(out=codes[:].bitcast(fmt), scales=scales[:], in_=src)
            return codes, scales

        dT = {}

        def move(h, g):
            dw = dq[h, g][:].rearrange("p c j -> p (c j)").bitcast(F32)
            dT[h, g] = ring.tile([P, 4, P, 4], BF16, name="dT", tag="dT", bufs=2, align_bytes=64)
            for jp in range(2):
                mv = psum.tile([P, 4, P], F32, name="mv", tag="mv", bufs=2)
                for k in range(4):
                    nc.tensor.transpose(mv[:, k, :], dw[:, 2 * P * k + jp : 2 * P * (k + 1) : 2], ident_f[:])
                nc.scalar.copy(out=dT[h, g][:, 2 * jp : 2 * jp + 2],
                               in_=mv[:].rearrange("p k n -> p (k n)").bitcast(BF16).rearrange("p (k n e) -> p e n k", k=4, e=2))

        def quant_tok(h, g):
            q1[h, g], q1s[h, g] = quant(dq[h, g][:].rearrange("p c j -> p (c j)"), E5, "q1", 5)

        def quant_unit(h, g):
            q0[h, g], q0s[h, g] = quant(dT[h, g][:].rearrange("p a b c -> p (a b c)"), E5, "q0", 6)

        def do_x(g):
            xi = ring.tile([P, F, 4], BF16, name="xi", tag="il", bufs=3, align_bytes=64)
            nc.gpsimd.tensor_scalar(out=xi[:], in0=x_sb[g][:].rearrange("p j f -> p f j"), scalar1=1.0, scalar2=0.0, op0=ALU.mult, op1=ALU.add)
            xq[g], xs[g] = quant(xi[:].rearrange("p f j -> p (f j)"), E4, "xq", 4)

        def w_ln(h, a_sb):
            inv[h] = keep.tile([P, 4, F], F32, name="inv%d" % h)
            nc.gpsimd.tensor_tensor(out=inv[h][:], in0=a_sb[:], in1=a_sb[:], op=ALU.mult)
            nc.scalar.activation(out=inv[h][:], in_=inv[h][:], func=ACT.Ln)

        def w_exp(h):
            nc.scalar.activation(out=inv[h][:], in_=inv[h][:], func=ACT.Exp, scale=-1.0)

        def w_q_(h):
            iv = inv[h][:].rearrange("p t f -> p f t")
            wi = ring.tile([P, F, 4], BF16, name="wi", tag="il", bufs=3, align_bytes=64)
            nc.vector.tensor_copy(out=wi[:], in_=iv)
            ws = ring.tile([P, F, 4], BF16, name="wi", tag="il", bufs=3, align_bytes=64)
            nc.vector.tensor_tensor(out=ws[:], in0=s_sb[h][:].rearrange("p t f -> p f t"), in1=iv, op=ALU.mult)
            w_q[h, 0], w_s[h, 0] = quant(wi[:].rearrange("p f t -> p (f t)"), E4, "wq", 4)
            w_q[h, 1], w_s[h, 1] = quant(ws[:].rearrange("p f t -> p (f t)"), E4, "wq", 4)

        def s_sum(h):
            ps = psum.tile([P, 4, P], F32, name="s_ps", tag="sum")
            for k in range(4):
                for i in range(16):
                    g, j = divmod(i, 4)
                    nc.tensor.matmul(ps[:, k, :], lhsT=tt_[h, g][:, j, k * P : (k + 1) * P], rhs=ident_f[:], is_transpose=True,
                                     start=(i == 0), stop=(i == 15))
            sv = ring.tile([P, 4], F32, name="sv", tag="sv", bufs=2)
            nc.vector.tensor_reduce(out=sv[:], in_=ps[:], axis=AX.X, op=ALU.add)
            nc.vector.tensor_tensor(out=sv[:], in0=sv[:], in1=f_col[:, 4 * h : 4 * h + 4], op=ALU.mult)
            return sv

        def out1(h, k, sv):
            acc = psum.tile([P, F], F32, name="acc", tag="acc", bufs=4)
            for g in range(NG):
                c = slice(k * P, (k + 1) * P)
                nc.tensor.matmul_mx(out=acc[:], lhsT=q1[h, g][:, c].bitcast(E5), lhsT_scale=q1s[h, g][:, c],
                                    rhs=xq[g][:].bitcast(E4), rhs_scale=xs[g][:], start=(g == 0), stop=(g == NG - 1))
            u = ring.tile([P, F], F32, name="u", tag="u", bufs=3)
            nc.vector.scalar_tensor_tensor(out=u[:], in0=s_sb[h][:, k, :], scalar=sv[:, k : k + 1], in1=acc[:], op0=ALU.mult, op1=ALU.add)
            o = ring.tile([P, F], F32, name="o1", tag="o1", bufs=3)
            nc.vector.scalar_tensor_tensor(out=o[:], in0=u[:], scalar=2.0, in1=inv[h][:, k, :], op0=ALU.mult, op1=ALU.mult)
            for e in range(2):
                nc.sync.dma_start(out=o1_v[h, e][:, k, :], in_=o[e:P:2, :])

        def out0(g):
            for j2 in range(2):
                o = ring.tile([P, 2, F], F32, name="o0", tag="o0", bufs=2)
                for j1 in range(2):
                    j = 2 * j2 + j1
                    c = slice(j * P, (j + 1) * P)
                    acc = []
                    for n in range(2):
                        a = psum.tile([P, F], F32, name="acc", tag="acc", bufs=4)
                        acc.append(a)
                        for h in range(NH):
                            nc.tensor.matmul_mx(out=a[:], lhsT=q0[h, g][:, c].bitcast(E5), lhsT_scale=q0s[h, g][:, c],
                                                rhs=w_q[h, n][:].bitcast(E4), rhs_scale=w_s[h, n][:], start=(h == 0), stop=(h == 1))
                    v = ring.tile([P, F], F32, name="v", tag="v", bufs=3)
                    nc.vector.scalar_tensor_tensor(out=v[:], in0=acc[0][:], scalar=2.0, in1=x_sb[g][:, j, :], op0=ALU.mult, op1=ALU.mult)
                    nc.vector.scalar_tensor_tensor(out=o[:, j1, :], in0=acc[1][:], scalar=2.0, in1=v[:], op0=ALU.mult, op1=ALU.add)
                nc.sync.dma_start(out=o0_v[g][:, 2 * j2 : 2 * j2 + 2, :], in_=o[:])

        load_chunk(0, 0)
        load_chunk(0, 1)
        load_x(0)
        a0 = load_w(0)
        a1 = load_w(1)
        load_x(1)
        spread_f(0)
        for g in range(NG):
            if g == 1:
                load_chunk(0, 2)
                load_x(2)
            if g == 2:
                load_chunk(0, 3)
                load_x(3)
            act_chunk(0, g)
            p1(0, g)
            do_x(g)
            p2(0, g)
            quant_tok(0, g)
            move(0, g)
            quant_unit(0, g)
            if g == 1:
                w_ln(0, a0)
                w_ln(1, a1)
                w_exp(0)
                w_exp(1)
            if g == 2:
                w_q_(0)
            if g == 3:
                w_q_(1)
        load_chunk(1, 0)
        spread_f(1)
        sv = s_sum(0)
        for k in range(4):
            out1(0, k, sv)
        for g in range(NG):
            if g + 1 < NG:
                load_chunk(1, g + 1)
            act_chunk(1, g)
            p1(1, g)
            p2(1, g)
            quant_tok(1, g)
            move(1, g)
            quant_unit(1, g)
            out0(g)
        sv = s_sum(1)
        for k in range(4):
            out1(1, k, sv)
